import numpy as np
import ml_dtypes

BF16 = ml_dtypes.bfloat16


def bf(x):
    return np.asarray(x, np.float32).astype(BF16)


def f32(x):
    return np.asarray(x, np.float32)


def f64(x):
    return np.asarray(x).astype(np.float64)


def striped(idx):
    return np.tile(idx.reshape(-1, 16).T, (8, 1))


C, S, Q, F, N = 128, 4096, 32, 32, 1024


def setup_inputs():
    x = f32(np.random.standard_normal((C, S)))
    kern = f32(np.tile(0.2 * np.random.standard_normal((1, N)), (C, 1)))
    bias = f32(np.tile(0.1 * np.random.standard_normal((1, Q)), (C, 1)))
    idx = np.random.permutation(np.tile(np.arange(S), 2))[:N]
    return {"x": x, "kern": kern, "bias": bias, "offs": striped(idx)}


def reference(x, kern, bias, offs):
    idx = offs[:16].T.reshape(-1)
    prod = f64(x)[:, idx] * f64(kern)
    return np.tanh(prod.reshape(C, Q, F).sum(axis=2) + f64(bias))

@@ -1,0 +1,44 @@
+import concourse.mybir as mybir
+
+SAMPLES = 128
+INPUT_NODES = 4096
+NODES = 32
+FAN_IN = 32
+CONNECTIONS = NODES * FAN_IN
+
+FLOPS = 2 * SAMPLES * CONNECTIONS
+
+F32 = mybir.dt.float32
+U16 = mybir.dt.uint16
+
+
+def tile_directencodingmodel_kernel(tc, x, kern, bias, offs, out):
+    nc = tc.nc
+    with tc.tile_pool(name="held", bufs=1) as held:
+        offsets = held.tile([SAMPLES, CONNECTIONS // 16], U16, name="offsets")
+        nc.sync.dma_start(offsets[:], offs)
+        table = held.tile([SAMPLES, INPUT_NODES], F32, name="table")
+        nc.sync.dma_start(table[:], x)
+        weights = held.tile([SAMPLES, CONNECTIONS], F32, name="weights")
+        nc.scalar.dma_start(weights[:], kern)
+        biases = held.tile([SAMPLES, NODES], F32, name="biases")
+        nc.scalar.dma_start(biases[:], bias)
+
+        prod = held.tile([SAMPLES, CONNECTIONS], F32, name="prod")
+        nc.vector.tensor_tensor(
+            prod[:], table[:].indirect(offsets[:]), weights[:], mybir.AluOpType.mult
+        )
+
+        sums = held.tile([SAMPLES, NODES], F32, name="sums")
+        nc.vector.tensor_reduce(
+            sums[:],
+            prod[:].rearrange("c (q f) -> c q f", f=FAN_IN),
+            axis=mybir.AxisListType.X,
+            op=mybir.AluOpType.add,
+        )
+        biased = held.tile([SAMPLES, NODES], F32, name="biased")
+        nc.vector.tensor_tensor(biased[:], sums[:], biases[:], mybir.AluOpType.add)
+
+        result = held.tile([SAMPLES, NODES], F32, name="result")
+        nc.scalar.activation(result[:], biased[:], mybir.ActivationFunctionType.Tanh)
+        nc.sync.dma_start(out, result[:])

@@ -6,6 +6,9 @@ NODES = 32
 FAN_IN = 32
 CONNECTIONS = NODES * FAN_IN
 
+PIECES = 4
+PIECE = CONNECTIONS // PIECES
+
 FLOPS = 2 * SAMPLES * CONNECTIONS
 
 F32 = mybir.dt.float32
@@ -15,19 +18,26 @@ U16 = mybir.dt.uint16
 def tile_directencodingmodel_kernel(tc, x, kern, bias, offs, out):
     nc = tc.nc
     with tc.tile_pool(name="held", bufs=1) as held:
-        offsets = held.tile([SAMPLES, CONNECTIONS // 16], U16, name="offsets")
-        nc.sync.dma_start(offsets[:], offs)
         table = held.tile([SAMPLES, INPUT_NODES], F32, name="table")
         nc.sync.dma_start(table[:], x)
-        weights = held.tile([SAMPLES, CONNECTIONS], F32, name="weights")
-        nc.scalar.dma_start(weights[:], kern)
+        offsets = held.tile([SAMPLES, CONNECTIONS // 16], U16, name="offsets")
+        nc.sync.dma_start(offsets[:], offs)
+        weights = [
+            held.tile([SAMPLES, PIECE], F32, name=f"weights{i}") for i in range(PIECES)
+        ]
+        for i in range(PIECES):
+            nc.sync.dma_start(weights[i][:], kern[:, i * PIECE : (i + 1) * PIECE])
         biases = held.tile([SAMPLES, NODES], F32, name="biases")
-        nc.scalar.dma_start(biases[:], bias)
+        nc.sync.dma_start(biases[:], bias)
 
         prod = held.tile([SAMPLES, CONNECTIONS], F32, name="prod")
-        nc.vector.tensor_tensor(
-            prod[:], table[:].indirect(offsets[:]), weights[:], mybir.AluOpType.mult
-        )
+        for i in range(PIECES):
+            nc.vector.tensor_tensor(
+                prod[:, i * PIECE : (i + 1) * PIECE],
+                table[:].indirect(offsets[:, i * (PIECE // 16) : (i + 1) * (PIECE // 16)]),
+                weights[i][:],
+                mybir.AluOpType.mult,
+            )
 
         sums = held.tile([SAMPLES, NODES], F32, name="sums")
         nc.vector.tensor_reduce(

@@ -5,9 +5,7 @@ INPUT_NODES = 4096
 NODES = 32
 FAN_IN = 32
 CONNECTIONS = NODES * FAN_IN
-
-PIECES = 4
-PIECE = CONNECTIONS // PIECES
+BANK = 512
 
 FLOPS = 2 * SAMPLES * CONNECTIONS
 
@@ -17,27 +15,31 @@ U16 = mybir.dt.uint16
 
 def tile_directencodingmodel_kernel(tc, x, kern, bias, offs, out):
     nc = tc.nc
-    with tc.tile_pool(name="held", bufs=1) as held:
-        table = held.tile([SAMPLES, INPUT_NODES], F32, name="table")
-        nc.sync.dma_start(table[:], x)
+    with (
+        tc.tile_pool(name="held", bufs=1) as held,
+        tc.psum_pool(name="psum", bufs=1) as psum,
+    ):
         offsets = held.tile([SAMPLES, CONNECTIONS // 16], U16, name="offsets")
         nc.sync.dma_start(offsets[:], offs)
-        weights = [
-            held.tile([SAMPLES, PIECE], F32, name=f"weights{i}") for i in range(PIECES)
-        ]
-        for i in range(PIECES):
-            nc.sync.dma_start(weights[i][:], kern[:, i * PIECE : (i + 1) * PIECE])
+        table = held.tile([SAMPLES, INPUT_NODES], F32, name="table")
+        nc.sync.dma_start(table[:], x)
+        kern_row = held.tile([1, CONNECTIONS], F32, name="kern_row")
+        nc.scalar.dma_start(kern_row[:], kern[0:1, :])
         biases = held.tile([SAMPLES, NODES], F32, name="biases")
-        nc.sync.dma_start(biases[:], bias)
+        nc.scalar.dma_start(biases[:], bias)
+
+        ones = held.tile([1, SAMPLES], F32, name="ones")
+        nc.vector.memset(ones[:], 1.0)
+        weights = held.tile([SAMPLES, CONNECTIONS], F32, name="weights")
+        for b in range(CONNECTIONS // BANK):
+            repeated = psum.tile([SAMPLES, BANK], F32, name=f"repeated{b}")
+            nc.tensor.matmul(repeated[:], ones[:], kern_row[:, b * BANK : (b + 1) * BANK])
+            nc.vector.tensor_copy(weights[:, b * BANK : (b + 1) * BANK], repeated[:])
 
         prod = held.tile([SAMPLES, CONNECTIONS], F32, name="prod")
-        for i in range(PIECES):
-            nc.vector.tensor_tensor(
-                prod[:, i * PIECE : (i + 1) * PIECE],
-                table[:].indirect(offsets[:, i * (PIECE // 16) : (i + 1) * (PIECE // 16)]),
-                weights[i][:],
-                mybir.AluOpType.mult,
-            )
+        nc.vector.tensor_tensor(
+            prod[:], table[:].indirect(offsets[:]), weights[:], mybir.AluOpType.mult
+        )
 
         sums = held.tile([SAMPLES, NODES], F32, name="sums")
         nc.vector.tensor_reduce(

@@ -5,7 +5,12 @@ INPUT_NODES = 4096
 NODES = 32
 FAN_IN = 32
 CONNECTIONS = NODES * FAN_IN
-BANK = 512
+
+PIECES = 4
+PIECE = CONNECTIONS // PIECES
+PIECE_NODES = NODES // PIECES
+SCALAR_PIECES = 2
+SCALAR_NODES = SCALAR_PIECES * PIECE_NODES
 
 FLOPS = 2 * SAMPLES * CONNECTIONS
 
@@ -15,36 +20,41 @@ U16 = mybir.dt.uint16
 
 def tile_directencodingmodel_kernel(tc, x, kern, bias, offs, out):
     nc = tc.nc
-    with (
-        tc.tile_pool(name="held", bufs=1) as held,
-        tc.psum_pool(name="psum", bufs=1) as psum,
-    ):
-        offsets = held.tile([SAMPLES, CONNECTIONS // 16], U16, name="offsets")
-        nc.sync.dma_start(offsets[:], offs)
+    with tc.tile_pool(name="held", bufs=1) as held:
         table = held.tile([SAMPLES, INPUT_NODES], F32, name="table")
         nc.sync.dma_start(table[:], x)
-        kern_row = held.tile([1, CONNECTIONS], F32, name="kern_row")
-        nc.scalar.dma_start(kern_row[:], kern[0:1, :])
+        offsets = held.tile([SAMPLES, CONNECTIONS // 16], U16, name="offsets")
+        nc.sync.dma_start(offsets[:], offs)
+        weights = [
+            held.tile([SAMPLES, PIECE], F32, name=f"weights{i}") for i in range(PIECES)
+        ]
+        for i in range(PIECES):
+            nc.sync.dma_start(weights[i][:], kern[:, i * PIECE : (i + 1) * PIECE])
         biases = held.tile([SAMPLES, NODES], F32, name="biases")
-        nc.scalar.dma_start(biases[:], bias)
-
-        ones = held.tile([1, SAMPLES], F32, name="ones")
-        nc.vector.memset(ones[:], 1.0)
-        weights = held.tile([SAMPLES, CONNECTIONS], F32, name="weights")
-        for b in range(CONNECTIONS // BANK):
-            repeated = psum.tile([SAMPLES, BANK], F32, name=f"repeated{b}")
-            nc.tensor.matmul(repeated[:], ones[:], kern_row[:, b * BANK : (b + 1) * BANK])
-            nc.vector.tensor_copy(weights[:, b * BANK : (b + 1) * BANK], repeated[:])
-
-        prod = held.tile([SAMPLES, CONNECTIONS], F32, name="prod")
-        nc.vector.tensor_tensor(
-            prod[:], table[:].indirect(offsets[:]), weights[:], mybir.AluOpType.mult
-        )
+        nc.sync.dma_start(biases[:], bias)
 
         sums = held.tile([SAMPLES, NODES], F32, name="sums")
+        prod = held.tile([SAMPLES, CONNECTIONS], F32, name="prod")
+        copied = held.tile([SAMPLES, SCALAR_NODES * FAN_IN], F32, name="copied")
+        for i in range(PIECES):
+            nc.vector.tensor_tensor(
+                prod[:, i * PIECE : (i + 1) * PIECE],
+                table[:].indirect(offsets[:, i * (PIECE // 16) : (i + 1) * (PIECE // 16)]),
+                weights[i][:],
+                mybir.AluOpType.mult,
+            )
+            if i < SCALAR_PIECES:
+                for q in range(i * PIECE_NODES, (i + 1) * PIECE_NODES):
+                    nc.scalar.activation(
+                        copied[:, q * FAN_IN : (q + 1) * FAN_IN],
+                        prod[:, q * FAN_IN : (q + 1) * FAN_IN],
+                        mybir.ActivationFunctionType.Copy,
+                        accum_out=sums[:, q : q + 1],
+                    )
+
         nc.vector.tensor_reduce(
-            sums[:],
-            prod[:].rearrange("c (q f) -> c q f", f=FAN_IN),
+            sums[:, SCALAR_NODES:],
+            prod[:, SCALAR_NODES * FAN_IN :].rearrange("c (q f) -> c q f", f=FAN_IN),
             axis=mybir.AxisListType.X,
             op=mybir.AluOpType.add,
         )

@@ -9,7 +9,7 @@ CONNECTIONS = NODES * FAN_IN
 PIECES = 4
 PIECE = CONNECTIONS // PIECES
 PIECE_NODES = NODES // PIECES
-SCALAR_PIECES = 2
+SCALAR_PIECES = 3
 SCALAR_NODES = SCALAR_PIECES * PIECE_NODES
 
 FLOPS = 2 * SAMPLES * CONNECTIONS

@@ -6,11 +6,10 @@ NODES = 32
 FAN_IN = 32
 CONNECTIONS = NODES * FAN_IN
 
-PIECES = 4
-PIECE = CONNECTIONS // PIECES
-PIECE_NODES = NODES // PIECES
-SCALAR_PIECES = 3
-SCALAR_NODES = SCALAR_PIECES * PIECE_NODES
+PIECE_NODES = (4, 8, 8, 12)
+PIECES = len(PIECE_NODES)
+FIRST_NODE = [sum(PIECE_NODES[:i]) for i in range(PIECES + 1)]
+SCALAR_NODES = FIRST_NODE[PIECES - 1]
 
 FLOPS = 2 * SAMPLES * CONNECTIONS
 
@@ -26,10 +25,13 @@ def tile_directencodingmodel_kernel(tc, x, kern, bias, offs, out):
         offsets = held.tile([SAMPLES, CONNECTIONS // 16], U16, name="offsets")
         nc.sync.dma_start(offsets[:], offs)
         weights = [
-            held.tile([SAMPLES, PIECE], F32, name=f"weights{i}") for i in range(PIECES)
+            held.tile([SAMPLES, PIECE_NODES[i] * FAN_IN], F32, name=f"weights{i}")
+            for i in range(PIECES)
         ]
         for i in range(PIECES):
-            nc.sync.dma_start(weights[i][:], kern[:, i * PIECE : (i + 1) * PIECE])
+            nc.sync.dma_start(
+                weights[i][:], kern[:, FIRST_NODE[i] * FAN_IN : FIRST_NODE[i + 1] * FAN_IN]
+            )
         biases = held.tile([SAMPLES, NODES], F32, name="biases")
         nc.sync.dma_start(biases[:], bias)
 
@@ -37,14 +39,15 @@ def tile_directencodingmodel_kernel(tc, x, kern, bias, offs, out):
         prod = held.tile([SAMPLES, CONNECTIONS], F32, name="prod")
         copied = held.tile([SAMPLES, SCALAR_NODES * FAN_IN], F32, name="copied")
         for i in range(PIECES):
+            first, last = FIRST_NODE[i] * FAN_IN, FIRST_NODE[i + 1] * FAN_IN
             nc.vector.tensor_tensor(
-                prod[:, i * PIECE : (i + 1) * PIECE],
-                table[:].indirect(offsets[:, i * (PIECE // 16) : (i + 1) * (PIECE // 16)]),
+                prod[:, first:last],
+                table[:].indirect(offsets[:, first // 16 : last // 16]),
                 weights[i][:],
                 mybir.AluOpType.mult,
             )
-            if i < SCALAR_PIECES:
-                for q in range(i * PIECE_NODES, (i + 1) * PIECE_NODES):
+            if i < PIECES - 1:
+                for q in range(FIRST_NODE[i], FIRST_NODE[i + 1]):
                     nc.scalar.activation(
                         copied[:, q * FAN_IN : (q + 1) * FAN_IN],
                         prod[:, q * FAN_IN : (q + 1) * FAN_IN],

@@ -6,10 +6,10 @@ NODES = 32
 FAN_IN = 32
 CONNECTIONS = NODES * FAN_IN
 
-PIECE_NODES = (4, 8, 8, 12)
+PIECE_NODES = (4, 10, 14, 4)
 PIECES = len(PIECE_NODES)
 FIRST_NODE = [sum(PIECE_NODES[:i]) for i in range(PIECES + 1)]
-SCALAR_NODES = FIRST_NODE[PIECES - 1]
+VECTOR_PIECE = 2
 
 FLOPS = 2 * SAMPLES * CONNECTIONS
 
@@ -32,12 +32,15 @@ def tile_directencodingmodel_kernel(tc, x, kern, bias, offs, out):
             nc.sync.dma_start(
                 weights[i][:], kern[:, FIRST_NODE[i] * FAN_IN : FIRST_NODE[i + 1] * FAN_IN]
             )
-        biases = held.tile([SAMPLES, NODES], F32, name="biases")
-        nc.sync.dma_start(biases[:], bias)
 
-        sums = held.tile([SAMPLES, NODES], F32, name="sums")
+        biases = held.tile([SAMPLES, NODES], F32, name="biases")
+        nc.scalar.dma_start(biases[:], bias)
+        bias_parts = held.tile([SAMPLES, NODES], F32, name="bias_parts")
+        nc.scalar.mul(bias_parts[:], biases[:], 1.0 / FAN_IN)
+
         prod = held.tile([SAMPLES, CONNECTIONS], F32, name="prod")
-        copied = held.tile([SAMPLES, SCALAR_NODES * FAN_IN], F32, name="copied")
+        shifted = held.tile([SAMPLES, CONNECTIONS], F32, name="shifted")
+        biased = held.tile([SAMPLES, NODES], F32, name="biased")
         for i in range(PIECES):
             first, last = FIRST_NODE[i] * FAN_IN, FIRST_NODE[i + 1] * FAN_IN
             nc.vector.tensor_tensor(
@@ -46,23 +49,27 @@ def tile_directencodingmodel_kernel(tc, x, kern, bias, offs, out):
                 weights[i][:],
                 mybir.AluOpType.mult,
             )
-            if i < PIECES - 1:
+            if i != VECTOR_PIECE:
                 for q in range(FIRST_NODE[i], FIRST_NODE[i + 1]):
                     nc.scalar.activation(
-                        copied[:, q * FAN_IN : (q + 1) * FAN_IN],
+                        shifted[:, q * FAN_IN : (q + 1) * FAN_IN],
                         prod[:, q * FAN_IN : (q + 1) * FAN_IN],
-                        mybir.ActivationFunctionType.Copy,
-                        accum_out=sums[:, q : q + 1],
+                        mybir.ActivationFunctionType.Identity,
+                        bias=bias_parts[:, q : q + 1],
+                        accum_out=biased[:, q : q + 1],
                     )
 
+        low, high = FIRST_NODE[VECTOR_PIECE], FIRST_NODE[VECTOR_PIECE + 1]
+        sums = held.tile([SAMPLES, high - low], F32, name="sums")
         nc.vector.tensor_reduce(
-            sums[:, SCALAR_NODES:],
-            prod[:, SCALAR_NODES * FAN_IN :].rearrange("c (q f) -> c q f", f=FAN_IN),
+            sums[:],
+            prod[:, low * FAN_IN : high * FAN_IN].rearrange("c (q f) -> c q f", f=FAN_IN),
             axis=mybir.AxisListType.X,
             op=mybir.AluOpType.add,
         )
-        biased = held.tile([SAMPLES, NODES], F32, name="biased")
-        nc.vector.tensor_tensor(biased[:], sums[:], biases[:], mybir.AluOpType.add)
+        nc.vector.tensor_tensor(
+            biased[:, low:high], sums[:], biases[:, low:high], mybir.AluOpType.add
+        )
 
         result = held.tile([SAMPLES, NODES], F32, name="result")
         nc.scalar.activation(result[:], biased[:], mybir.ActivationFunctionType.Tanh)

@@ -28,13 +28,13 @@ def tile_directencodingmodel_kernel(tc, x, kern, bias, offs, out):
             held.tile([SAMPLES, PIECE_NODES[i] * FAN_IN], F32, name=f"weights{i}")
             for i in range(PIECES)
         ]
+        biases = held.tile([SAMPLES, NODES], F32, name="biases")
         for i in range(PIECES):
             nc.sync.dma_start(
                 weights[i][:], kern[:, FIRST_NODE[i] * FAN_IN : FIRST_NODE[i + 1] * FAN_IN]
             )
-
-        biases = held.tile([SAMPLES, NODES], F32, name="biases")
-        nc.scalar.dma_start(biases[:], bias)
+            if i == 1:
+                nc.sync.dma_start(biases[:], bias)
         bias_parts = held.tile([SAMPLES, NODES], F32, name="bias_parts")
         nc.scalar.mul(bias_parts[:], biases[:], 1.0 / FAN_IN)
 

@@ -6,15 +6,19 @@ NODES = 32
 FAN_IN = 32
 CONNECTIONS = NODES * FAN_IN
 
-PIECE_NODES = (4, 10, 14, 4)
+PIECE_NODES = (4, 8, 16, 4)
 PIECES = len(PIECE_NODES)
 FIRST_NODE = [sum(PIECE_NODES[:i]) for i in range(PIECES + 1)]
-VECTOR_PIECE = 2
+LAST_PIECE_NODE = FIRST_NODE[PIECES - 1]
+
+MIDDLE = (16, 24)
+SCALAR_SUMS = [q for q in range(LAST_PIECE_NODE) if not MIDDLE[0] <= q < MIDDLE[1]]
 
 FLOPS = 2 * SAMPLES * CONNECTIONS
 
 F32 = mybir.dt.float32
 U16 = mybir.dt.uint16
+ADD = mybir.AluOpType.add
 
 
 def tile_directencodingmodel_kernel(tc, x, kern, bias, offs, out):
@@ -35,10 +39,20 @@ def tile_directencodingmodel_kernel(tc, x, kern, bias, offs, out):
             )
             if i == 1:
                 nc.sync.dma_start(biases[:], bias)
+
+        prod = held.tile(
+            [SAMPLES, CONNECTIONS + PIECE_NODES[PIECES - 1] * FAN_IN], F32, name="prod"
+        )
         bias_parts = held.tile([SAMPLES, NODES], F32, name="bias_parts")
         nc.scalar.mul(bias_parts[:], biases[:], 1.0 / FAN_IN)
+        nc.scalar.mul(
+            prod[:, CONNECTIONS:].rearrange("c (q f) -> c q f", f=FAN_IN),
+            biases[:, LAST_PIECE_NODE:]
+            .unsqueeze(2)
+            .to_broadcast([SAMPLES, PIECE_NODES[PIECES - 1], FAN_IN]),
+            1.0 / FAN_IN,
+        )
 
-        prod = held.tile([SAMPLES, CONNECTIONS], F32, name="prod")
         shifted = held.tile([SAMPLES, CONNECTIONS], F32, name="shifted")
         biased = held.tile([SAMPLES, NODES], F32, name="biased")
         for i in range(PIECES):
@@ -49,27 +63,34 @@ def tile_directencodingmodel_kernel(tc, x, kern, bias, offs, out):
                 weights[i][:],
                 mybir.AluOpType.mult,
             )
-            if i != VECTOR_PIECE:
-                for q in range(FIRST_NODE[i], FIRST_NODE[i + 1]):
-                    nc.scalar.activation(
-                        shifted[:, q * FAN_IN : (q + 1) * FAN_IN],
-                        prod[:, q * FAN_IN : (q + 1) * FAN_IN],
-                        mybir.ActivationFunctionType.Identity,
-                        bias=bias_parts[:, q : q + 1],
-                        accum_out=biased[:, q : q + 1],
-                    )
+            for q in SCALAR_SUMS:
+                if not FIRST_NODE[i] <= q < FIRST_NODE[i + 1]:
+                    continue
+                nc.scalar.activation(
+                    shifted[:, q * FAN_IN : (q + 1) * FAN_IN],
+                    prod[:, q * FAN_IN : (q + 1) * FAN_IN],
+                    mybir.ActivationFunctionType.Identity,
+                    bias=bias_parts[:, q : q + 1],
+                    accum_out=biased[:, q : q + 1],
+                )
 
-        low, high = FIRST_NODE[VECTOR_PIECE], FIRST_NODE[VECTOR_PIECE + 1]
+        low, high = MIDDLE
         sums = held.tile([SAMPLES, high - low], F32, name="sums")
         nc.vector.tensor_reduce(
             sums[:],
             prod[:, low * FAN_IN : high * FAN_IN].rearrange("c (q f) -> c q f", f=FAN_IN),
             axis=mybir.AxisListType.X,
-            op=mybir.AluOpType.add,
+            op=ADD,
         )
-        nc.vector.tensor_tensor(
-            biased[:, low:high], sums[:], biases[:, low:high], mybir.AluOpType.add
+        nc.vector.tensor_reduce(
+            biased[:, LAST_PIECE_NODE:],
+            prod[:, LAST_PIECE_NODE * FAN_IN :].rearrange(
+                "c (s q f) -> c q s f", s=2, f=FAN_IN
+            ),
+            axis=mybir.AxisListType.XY,
+            op=ADD,
         )
+        nc.gpsimd.tensor_tensor(biased[:, low:high], sums[:], biases[:, low:high], ADD)
 
         result = held.tile([SAMPLES, NODES], F32, name="result")
         nc.scalar.activation(result[:], biased[:], mybir.ActivationFunctionType.Tanh)

@@ -6,13 +6,14 @@ NODES = 32
 FAN_IN = 32
 CONNECTIONS = NODES * FAN_IN
 
-PIECE_NODES = (4, 8, 16, 4)
+PIECE_NODES = (4, 10, 14, 4)
 PIECES = len(PIECE_NODES)
 FIRST_NODE = [sum(PIECE_NODES[:i]) for i in range(PIECES + 1)]
-LAST_PIECE_NODE = FIRST_NODE[PIECES - 1]
 
-MIDDLE = (16, 24)
-SCALAR_SUMS = [q for q in range(LAST_PIECE_NODE) if not MIDDLE[0] <= q < MIDDLE[1]]
+SCALAR_PLAIN = 16
+VECTOR_PLAIN = 24
+SCALAR_BIASED = 29
+VECTOR_BIASED_NODES = NODES - SCALAR_BIASED
 
 FLOPS = 2 * SAMPLES * CONNECTIONS
 
@@ -41,19 +42,20 @@ def tile_directencodingmodel_kernel(tc, x, kern, bias, offs, out):
                 nc.sync.dma_start(biases[:], bias)
 
         prod = held.tile(
-            [SAMPLES, CONNECTIONS + PIECE_NODES[PIECES - 1] * FAN_IN], F32, name="prod"
+            [SAMPLES, CONNECTIONS + VECTOR_BIASED_NODES * FAN_IN], F32, name="prod"
         )
         bias_parts = held.tile([SAMPLES, NODES], F32, name="bias_parts")
         nc.scalar.mul(bias_parts[:], biases[:], 1.0 / FAN_IN)
         nc.scalar.mul(
             prod[:, CONNECTIONS:].rearrange("c (q f) -> c q f", f=FAN_IN),
-            biases[:, LAST_PIECE_NODE:]
+            biases[:, SCALAR_BIASED:]
             .unsqueeze(2)
-            .to_broadcast([SAMPLES, PIECE_NODES[PIECES - 1], FAN_IN]),
+            .to_broadcast([SAMPLES, VECTOR_BIASED_NODES, FAN_IN]),
             1.0 / FAN_IN,
         )
 
-        shifted = held.tile([SAMPLES, CONNECTIONS], F32, name="shifted")
+        copied = held.tile([SAMPLES, CONNECTIONS], F32, name="copied")
+        sums = held.tile([SAMPLES, VECTOR_PLAIN], F32, name="sums")
         biased = held.tile([SAMPLES, NODES], F32, name="biased")
         for i in range(PIECES):
             first, last = FIRST_NODE[i] * FAN_IN, FIRST_NODE[i + 1] * FAN_IN
@@ -63,34 +65,43 @@ def tile_directencodingmodel_kernel(tc, x, kern, bias, offs, out):
                 weights[i][:],
                 mybir.AluOpType.mult,
             )
-            for q in SCALAR_SUMS:
-                if not FIRST_NODE[i] <= q < FIRST_NODE[i + 1]:
-                    continue
-                nc.scalar.activation(
-                    shifted[:, q * FAN_IN : (q + 1) * FAN_IN],
-                    prod[:, q * FAN_IN : (q + 1) * FAN_IN],
-                    mybir.ActivationFunctionType.Identity,
-                    bias=bias_parts[:, q : q + 1],
-                    accum_out=biased[:, q : q + 1],
-                )
+            for q in range(FIRST_NODE[i], min(FIRST_NODE[i + 1], SCALAR_BIASED)):
+                run = slice(q * FAN_IN, (q + 1) * FAN_IN)
+                if q < SCALAR_PLAIN:
+                    nc.scalar.activation(
+                        copied[:, run],
+                        prod[:, run],
+                        mybir.ActivationFunctionType.Copy,
+                        accum_out=sums[:, q : q + 1],
+                    )
+                elif q >= VECTOR_PLAIN:
+                    nc.scalar.activation(
+                        copied[:, run],
+                        prod[:, run],
+                        mybir.ActivationFunctionType.Identity,
+                        bias=bias_parts[:, q : q + 1],
+                        accum_out=biased[:, q : q + 1],
+                    )
 
-        low, high = MIDDLE
-        sums = held.tile([SAMPLES, high - low], F32, name="sums")
         nc.vector.tensor_reduce(
-            sums[:],
-            prod[:, low * FAN_IN : high * FAN_IN].rearrange("c (q f) -> c q f", f=FAN_IN),
+            sums[:, SCALAR_PLAIN:],
+            prod[:, SCALAR_PLAIN * FAN_IN : VECTOR_PLAIN * FAN_IN].rearrange(
+                "c (q f) -> c q f", f=FAN_IN
+            ),
             axis=mybir.AxisListType.X,
             op=ADD,
         )
         nc.vector.tensor_reduce(
-            biased[:, LAST_PIECE_NODE:],
-            prod[:, LAST_PIECE_NODE * FAN_IN :].rearrange(
+            biased[:, SCALAR_BIASED:],
+            prod[:, SCALAR_BIASED * FAN_IN :].rearrange(
                 "c (s q f) -> c q s f", s=2, f=FAN_IN
             ),
             axis=mybir.AxisListType.XY,
             op=ADD,
         )
-        nc.gpsimd.tensor_tensor(biased[:, low:high], sums[:], biases[:, low:high], ADD)
+        nc.vector.tensor_tensor(
+            biased[:, :VECTOR_PLAIN], sums[:], biases[:, :VECTOR_PLAIN], ADD
+        )
 
         result = held.tile([SAMPLES, NODES], F32, name="result")
         nc.scalar.activation(result[:], biased[:], mybir.ActivationFunctionType.Tanh)

@@ -10,10 +10,8 @@ PIECE_NODES = (4, 10, 14, 4)
 PIECES = len(PIECE_NODES)
 FIRST_NODE = [sum(PIECE_NODES[:i]) for i in range(PIECES + 1)]
 
-SCALAR_PLAIN = 16
-VECTOR_PLAIN = 24
-SCALAR_BIASED = 29
-VECTOR_BIASED_NODES = NODES - SCALAR_BIASED
+SCALAR_NODES = 18
+PLAIN_NODES = NODES - PIECE_NODES[PIECES - 1]
 
 FLOPS = 2 * SAMPLES * CONNECTIONS
 
@@ -42,20 +40,18 @@ def tile_directencodingmodel_kernel(tc, x, kern, bias, offs, out):
                 nc.sync.dma_start(biases[:], bias)
 
         prod = held.tile(
-            [SAMPLES, CONNECTIONS + VECTOR_BIASED_NODES * FAN_IN], F32, name="prod"
+            [SAMPLES, CONNECTIONS + PIECE_NODES[PIECES - 1] * FAN_IN], F32, name="prod"
         )
-        bias_parts = held.tile([SAMPLES, NODES], F32, name="bias_parts")
-        nc.scalar.mul(bias_parts[:], biases[:], 1.0 / FAN_IN)
         nc.scalar.mul(
             prod[:, CONNECTIONS:].rearrange("c (q f) -> c q f", f=FAN_IN),
-            biases[:, SCALAR_BIASED:]
+            biases[:, PLAIN_NODES:]
             .unsqueeze(2)
-            .to_broadcast([SAMPLES, VECTOR_BIASED_NODES, FAN_IN]),
+            .to_broadcast([SAMPLES, PIECE_NODES[PIECES - 1], FAN_IN]),
             1.0 / FAN_IN,
         )
 
-        copied = held.tile([SAMPLES, CONNECTIONS], F32, name="copied")
-        sums = held.tile([SAMPLES, VECTOR_PLAIN], F32, name="sums")
+        copied = held.tile([SAMPLES, SCALAR_NODES * FAN_IN], F32, name="copied")
+        sums = held.tile([SAMPLES, PLAIN_NODES], F32, name="sums")
         biased = held.tile([SAMPLES, NODES], F32, name="biased")
         for i in range(PIECES):
             first, last = FIRST_NODE[i] * FAN_IN, FIRST_NODE[i + 1] * FAN_IN
@@ -65,42 +61,39 @@ def tile_directencodingmodel_kernel(tc, x, kern, bias, offs, out):
                 weights[i][:],
                 mybir.AluOpType.mult,
             )
-            for q in range(FIRST_NODE[i], min(FIRST_NODE[i + 1], SCALAR_BIASED)):
+            for q in range(FIRST_NODE[i], min(FIRST_NODE[i + 1], SCALAR_NODES)):
                 run = slice(q * FAN_IN, (q + 1) * FAN_IN)
-                if q < SCALAR_PLAIN:
-                    nc.scalar.activation(
-                        copied[:, run],
-                        prod[:, run],
-                        mybir.ActivationFunctionType.Copy,
-                        accum_out=sums[:, q : q + 1],
-                    )
-                elif q >= VECTOR_PLAIN:
-                    nc.scalar.activation(
-                        copied[:, run],
-                        prod[:, run],
-                        mybir.ActivationFunctionType.Identity,
-                        bias=bias_parts[:, q : q + 1],
-                        accum_out=biased[:, q : q + 1],
-                    )
+                nc.scalar.activation(
+                    copied[:, run],
+                    prod[:, run],
+                    mybir.ActivationFunctionType.Copy,
+                    accum_out=sums[:, q : q + 1],
+                )
+        early_tanh = held.tile([SAMPLES, 1], F32, name="early_tanh")
+        nc.scalar.activation(
+            early_tanh[:],
+            sums[:, SCALAR_NODES - 1 : SCALAR_NODES],
+            mybir.ActivationFunctionType.Tanh,
+        )
 
         nc.vector.tensor_reduce(
-            sums[:, SCALAR_PLAIN:],
-            prod[:, SCALAR_PLAIN * FAN_IN : VECTOR_PLAIN * FAN_IN].rearrange(
+            sums[:, SCALAR_NODES:],
+            prod[:, SCALAR_NODES * FAN_IN : PLAIN_NODES * FAN_IN].rearrange(
                 "c (q f) -> c q f", f=FAN_IN
             ),
             axis=mybir.AxisListType.X,
             op=ADD,
         )
         nc.vector.tensor_reduce(
-            biased[:, SCALAR_BIASED:],
-            prod[:, SCALAR_BIASED * FAN_IN :].rearrange(
+            biased[:, PLAIN_NODES:],
+            prod[:, PLAIN_NODES * FAN_IN :].rearrange(
                 "c (s q f) -> c q s f", s=2, f=FAN_IN
             ),
             axis=mybir.AxisListType.XY,
             op=ADD,
         )
         nc.vector.tensor_tensor(
-            biased[:, :VECTOR_PLAIN], sums[:], biases[:, :VECTOR_PLAIN], ADD
+            biased[:, :PLAIN_NODES], sums[:], biases[:, :PLAIN_NODES], ADD
         )
 
         result = held.tile([SAMPLES, NODES], F32, name="result")

@@ -69,12 +69,6 @@ def tile_directencodingmodel_kernel(tc, x, kern, bias, offs, out):
                     mybir.ActivationFunctionType.Copy,
                     accum_out=sums[:, q : q + 1],
                 )
-        early_tanh = held.tile([SAMPLES, 1], F32, name="early_tanh")
-        nc.scalar.activation(
-            early_tanh[:],
-            sums[:, SCALAR_NODES - 1 : SCALAR_NODES],
-            mybir.ActivationFunctionType.Tanh,
-        )
 
         nc.vector.tensor_reduce(
             sums[:, SCALAR_NODES:],

@@ -10,7 +10,7 @@ PIECE_NODES = (4, 10, 14, 4)
 PIECES = len(PIECE_NODES)
 FIRST_NODE = [sum(PIECE_NODES[:i]) for i in range(PIECES + 1)]
 
-SCALAR_NODES = 18
+SCALAR_NODES = 20
 PLAIN_NODES = NODES - PIECE_NODES[PIECES - 1]
 
 FLOPS = 2 * SAMPLES * CONNECTIONS

@@ -23,10 +23,10 @@ ADD = mybir.AluOpType.add
 def tile_directencodingmodel_kernel(tc, x, kern, bias, offs, out):
     nc = tc.nc
     with tc.tile_pool(name="held", bufs=1) as held:
-        table = held.tile([SAMPLES, INPUT_NODES], F32, name="table")
-        nc.sync.dma_start(table[:], x)
         offsets = held.tile([SAMPLES, CONNECTIONS // 16], U16, name="offsets")
         nc.sync.dma_start(offsets[:], offs)
+        table = held.tile([SAMPLES, INPUT_NODES], F32, name="table")
+        nc.sync.dma_start(table[:], x)
         weights = [
             held.tile([SAMPLES, PIECE_NODES[i] * FAN_IN], F32, name=f"weights{i}")
             for i in range(PIECES)

import concourse.mybir as mybir

SAMPLES = 128
INPUT_NODES = 4096
NODES = 32
FAN_IN = 32
CONNECTIONS = NODES * FAN_IN

PIECE_NODES = (4, 10, 14, 4)
PIECES = len(PIECE_NODES)
FIRST_NODE = [sum(PIECE_NODES[:i]) for i in range(PIECES + 1)]

SCALAR_NODES = 20
PLAIN_NODES = NODES - PIECE_NODES[PIECES - 1]

FLOPS = 2 * SAMPLES * CONNECTIONS

F32 = mybir.dt.float32
U16 = mybir.dt.uint16
ADD = mybir.AluOpType.add


def tile_directencodingmodel_kernel(tc, x, kern, bias, offs, out):
    nc = tc.nc
    with tc.tile_pool(name="held", bufs=1) as held:
        offsets = held.tile([SAMPLES, CONNECTIONS // 16], U16, name="offsets")
        nc.sync.dma_start(offsets[:], offs)
        table = held.tile([SAMPLES, INPUT_NODES], F32, name="table")
        nc.sync.dma_start(table[:], x)
        weights = [
            held.tile([SAMPLES, PIECE_NODES[i] * FAN_IN], F32, name=f"weights{i}")
            for i in range(PIECES)
        ]
        biases = held.tile([SAMPLES, NODES], F32, name="biases")
        for i in range(PIECES):
            nc.sync.dma_start(
                weights[i][:], kern[:, FIRST_NODE[i] * FAN_IN : FIRST_NODE[i + 1] * FAN_IN]
            )
            if i == 1:
                nc.sync.dma_start(biases[:], bias)

        prod = held.tile(
            [SAMPLES, CONNECTIONS + PIECE_NODES[PIECES - 1] * FAN_IN], F32, name="prod"
        )
        nc.scalar.mul(
            prod[:, CONNECTIONS:].rearrange("c (q f) -> c q f", f=FAN_IN),
            biases[:, PLAIN_NODES:]
            .unsqueeze(2)
            .to_broadcast([SAMPLES, PIECE_NODES[PIECES - 1], FAN_IN]),
            1.0 / FAN_IN,
        )

        copied = held.tile([SAMPLES, SCALAR_NODES * FAN_IN], F32, name="copied")
        sums = held.tile([SAMPLES, PLAIN_NODES], F32, name="sums")
        biased = held.tile([SAMPLES, NODES], F32, name="biased")
        for i in range(PIECES):
            first, last = FIRST_NODE[i] * FAN_IN, FIRST_NODE[i + 1] * FAN_IN
            nc.vector.tensor_tensor(
                prod[:, first:last],
                table[:].indirect(offsets[:, first // 16 : last // 16]),
                weights[i][:],
                mybir.AluOpType.mult,
            )
            for q in range(FIRST_NODE[i], min(FIRST_NODE[i + 1], SCALAR_NODES)):
                run = slice(q * FAN_IN, (q + 1) * FAN_IN)
                nc.scalar.activation(
                    copied[:, run],
                    prod[:, run],
                    mybir.ActivationFunctionType.Copy,
                    accum_out=sums[:, q : q + 1],
                )

        nc.vector.tensor_reduce(
            sums[:, SCALAR_NODES:],
            prod[:, SCALAR_NODES * FAN_IN : PLAIN_NODES * FAN_IN].rearrange(
                "c (q f) -> c q f", f=FAN_IN
            ),
            axis=mybir.AxisListType.X,
            op=ADD,
        )
        nc.vector.tensor_reduce(
            biased[:, PLAIN_NODES:],
            prod[:, PLAIN_NODES * FAN_IN :].rearrange(
                "c (s q f) -> c q s f", s=2, f=FAN_IN
            ),
            axis=mybir.AxisListType.XY,
            op=ADD,
        )
        nc.vector.tensor_tensor(
            biased[:, :PLAIN_NODES], sums[:], biases[:, :PLAIN_NODES], ADD
        )

        result = held.tile([SAMPLES, NODES], F32, name="result")
        nc.scalar.activation(result[:], biased[:], mybir.ActivationFunctionType.Tanh)
        nc.sync.dma_start(out, result[:])
